import numpy as np
import ml_dtypes


def mxq(x, axis, fmt="e4m3"):
    dtype, down = {"e4m3": (ml_dtypes.float8_e4m3fn, 7), "e5m2": (ml_dtypes.float8_e5m2, 14)}[fmt]
    v = np.moveaxis(np.asarray(x, np.float32).astype(ml_dtypes.bfloat16).astype(np.float64), axis, -1)
    blocks = v.reshape(v.shape[:-1] + (-1, 32))
    amax = np.abs(blocks).max(-1, keepdims=True)
    byte = np.maximum(np.where(amax > 0, np.frexp(amax)[1] - 1 + 127, 0) - down, 1)
    scale = np.exp2(byte - 127.0)
    codes = (blocks / scale).astype(np.float32).astype(dtype).astype(np.float64)
    return np.moveaxis((codes * scale).reshape(v.shape), -1, axis)


WIDE = False


def mx_kscale(k):
    if not WIDE:
        return np.ones(k)
    levels = np.array([10, -10, 5, -5, 0])
    a = np.random.permutation(np.resize(levels, k // 512 * 4)).reshape(k // 512, 4)
    idx = np.arange(k)
    return np.exp2(a[idx // 512, idx % 128 // 32])


BF16 = ml_dtypes.bfloat16


def bf(x):
    return np.asarray(x, np.float32).astype(BF16)


def f64(x):
    return np.asarray(x).astype(np.float64)


E2M1 = np.array([0.0, 0.5, 1.0, 1.5, 2.0, 3.0, 4.0, 6.0, -0.0, -0.5, -1.0, -1.5, -2.0, -3.0, -4.0, -6.0])


def pack_weight(w, fmt):
    k, n = w.shape
    w = f64(bf(w)).reshape(k // 32, 32, n)
    amax = np.abs(w).max(1)
    if fmt == "e4m3":
        byte = np.frexp(amax)[1] - 1 + 127 - 7
    else:
        mant, ex = np.frexp(amax / 6.0)
        byte = np.where(mant > 0.5, ex, ex - 1) + 127
    byte = np.clip(np.where(amax > 0, byte, 1), 1, 254)
    scaled = (w * np.exp2(127.0 - byte)[:, None, :]).reshape(k, n).astype(np.float32)
    by_word = np.ascontiguousarray(scaled.reshape(k // 512, 128, 4, n).transpose(0, 1, 3, 2))
    if fmt == "e4m3":
        words = by_word.astype(ml_dtypes.float8_e4m3fn).view(np.uint8)
    else:
        c = by_word.astype(ml_dtypes.float4_e2m1fn).view(np.uint8) & 0xF
        words = c[..., 0::2] | (c[..., 1::2] << 4)
    return np.ascontiguousarray(words), np.ascontiguousarray(byte.astype(np.uint8).reshape(k // 512, 16, n))


def unpack_weight(words, scales, fmt):
    g, p, n, _ = words.shape
    if fmt == "e4m3":
        vals = np.ascontiguousarray(words).view(ml_dtypes.float8_e4m3fn).astype(np.float64)
    else:
        nib = np.empty((g, p, n, 4), np.uint8)
        nib[..., 0::2] = words & 0xF
        nib[..., 1::2] = words >> 4
        vals = E2M1[nib]
    vals = vals * np.repeat(np.exp2(scales.astype(np.float64) - 127.0), 8, axis=1)[..., None]
    return vals.transpose(0, 1, 3, 2).reshape(g * 512, n)


B, S, D, H, DH, F = 2, 64, 8192, 16, 64, 4096
E = H * DH
EPS = 1e-5
FMT = "e4m3"


def layernorm(x, g, b):
    mu = x.mean(-1, keepdims=True)
    var = np.square(x - mu).mean(-1, keepdims=True)
    return (x - mu) / np.sqrt(var + EPS) * g + b


def make_pe():
    position = np.arange(S)[:, None] * 1.0
    div_term = np.exp(np.arange(0, DH, 2) * -(np.log(10000.0) / DH))
    pe = np.zeros((S, DH))
    pe[:, 0::2] = np.sin(position * div_term)
    pe[:, 1::2] = np.cos(position * div_term)
    return pe


def rope(t, pe):
    tr = t.reshape(B, H, S, DH // 2, 2)
    c = pe[:S, 0::2][None, None]
    d = pe[:S, 1::2][None, None]
    t0 = tr[..., 0] * c - tr[..., 1] * d
    t1 = tr[..., 0] * d + tr[..., 1] * c
    return np.stack([t0, t1], axis=-1).reshape(B, H, S, DH)


def setup_inputs():
    s = mx_kscale(D)
    x = np.random.standard_normal((B, S, D)) + 0.5 * np.random.standard_normal((B, S, 1))
    w_qkv = np.random.standard_normal((3 * E, D)) / np.sqrt(D) / s
    words, scales = pack_weight(w_qkv.T, FMT)
    return {"x": bf(x),
            "pe": bf(make_pe()),
            "w_qkv_words": words,
            "w_qkv_scales": scales,
            "g1": bf((1.0 + 0.1 * np.random.standard_normal(D)) * s),
            "b1": bf(0.1 * np.random.standard_normal(D) * s)}


def reference(x, pe, w_qkv_words, w_qkv_scales, g1, b1):
    h = layernorm(f64(x), f64(g1), f64(b1))
    qkv = mxq(h, 2, "e4m3") @ unpack_weight(w_qkv_words, w_qkv_scales, FMT)
    qkv = qkv.reshape(B, S, 3, H, DH)
    q, k, v = [qkv[:, :, i].transpose(0, 2, 1, 3) for i in range(3)]
    p = f64(pe)
    return rope(q, p), rope(k, p), v

@@ -1,0 +1,255 @@
+from contextlib import ExitStack
+
+import concourse.mybir as mybir
+from concourse.masks import make_identity
+
+F32 = mybir.dt.float32
+BF16 = mybir.dt.bfloat16
+I32 = mybir.dt.int32
+U32 = mybir.dt.uint32
+U8 = mybir.dt.uint8
+FP8X4 = mybir.dt.float8_e4m3fn_x4
+ALU = mybir.AluOpType
+ACT = mybir.ActivationFunctionType
+
+P = 128
+PACK = 4
+K_PASS = P * PACK
+BATCH, SEQ, D = 2, 64, 8192
+HEADS, DH = 16, 64
+PAIRS = DH // 2
+GROUPS = D // K_PASS
+EPS = 1e-5
+
+BANK = 512
+BANK_HEADS = BANK // DH
+QK_BANKS = 2 * HEADS * DH // BANK
+V_BANKS = HEADS * DH // BANK
+N_COLS = (QK_BANKS + V_BANKS) * BANK
+
+SCALE_ROWS = 4
+QUADRANTS = 4
+SHARE = 4
+X_PIECES = 4
+BN_STATS_DIM = 6
+QK_BUFS = 10
+
+FLOPS = 2 * P * D * N_COLS
+
+
+def tile_minitransformerlayer_pa_k_kernel(
+    tc, x, pe, w_qkv_words, w_qkv_scales, g1, b1, out_0, out_1, out_2
+):
+    nc = tc.nc
+    outs = (out_0, out_1, out_2)
+
+    with ExitStack() as ctx:
+        keep = ctx.enter_context(tc.tile_pool(name="keep", bufs=1))
+        stage = ctx.enter_context(tc.tile_pool(name="stage", bufs=2))
+        qk_pool = ctx.enter_context(tc.tile_pool(name="qk_words", bufs=QK_BUFS))
+        v_pool = ctx.enter_context(tc.tile_pool(name="v_words", bufs=GROUPS))
+        acc_pool = ctx.enter_context(tc.psum_pool(name="acc", bufs=1))
+        flip_pool = ctx.enter_context(tc.psum_pool(name="flip", bufs=2))
+        ctx.enter_context(tc.manual_schedule())
+
+        gb_rows = keep.tile([P, K_PASS], BF16)
+        nc.vector.memset(gb_rows[:], 0.0)
+        w_planes = keep.tile([P, GROUPS // SHARE, N_COLS], U8, align_bytes=64)
+        nc.vector.memset(w_planes[:].bitcast(I32), 0)
+
+        identity = keep.tile([P, P], F32)
+        make_identity(nc, identity[:])
+
+        x_rows = x.flatten_outer_dims()
+        x_sb = keep.tile([P, D], BF16)
+        for piece in range(X_PIECES):
+            cols = slice(piece * D // X_PIECES, (piece + 1) * D // X_PIECES)
+            nc.sync.dma_start(out=x_sb[:, cols], in_=x_rows[:, cols])
+
+        nc.scalar.dma_start(out=gb_rows[0:GROUPS, :], in_=g1.rearrange("(g k) -> g k", k=K_PASS))
+        nc.scalar.dma_start(
+            out=gb_rows[GROUPS : 2 * GROUPS, :], in_=b1.rearrange("(g k) -> g k", k=K_PASS)
+        )
+        pe_sb = keep.tile([P, DH], BF16)
+        for b in range(BATCH):
+            nc.scalar.dma_start(out=pe_sb[b * SEQ : (b + 1) * SEQ, :], in_=pe)
+
+        scale_words = w_qkv_scales.bitcast(I32)
+        for a in range(GROUPS // SHARE):
+            for quadrant in range(QUADRANTS):
+                first = 32 * quadrant
+                nc.sync.dma_start(
+                    out=w_planes[first : first + SHARE * SCALE_ROWS, a, :].bitcast(I32),
+                    in_=scale_words[
+                        SHARE * a : SHARE * (a + 1),
+                        SCALE_ROWS * quadrant : SCALE_ROWS * (quadrant + 1),
+                        :,
+                    ],
+                )
+
+        def load_words(pool, g, first_col, n_cols):
+            words = pool.tile([P, n_cols], U32, align_bytes=64)
+            source = w_qkv_words[g].rearrange("p n t -> p (n t)")
+            source = source[:, PACK * first_col : PACK * (first_col + n_cols)]
+            nc.sync.dma_start(out=words[:].bitcast(I32), in_=source.bitcast(I32))
+            return words
+
+        qk_words = [load_words(qk_pool, g, 0, QK_BANKS * BANK) for g in range(GROUPS)]
+        v_words = [load_words(v_pool, g, QK_BANKS * BANK, V_BANKS * BANK) for g in range(GROUPS)]
+
+        stats = keep.tile([P, GROUPS, BN_STATS_DIM], F32)
+        for g in range(GROUPS):
+            nc.vector.bn_stats(out=stats[:, g, :], in_=x_sb[:, g * K_PASS : (g + 1) * K_PASS])
+        mean_var = keep.tile([P, 2], F32)
+        nc.vector.bn_aggr(out=mean_var[:], in_=stats[:].rearrange("p g s -> p (g s)"))
+        var_eps = keep.tile([P, 1], F32)
+        nc.vector.tensor_scalar(
+            out=var_eps[:], in0=mean_var[:, 1:2], scalar1=EPS, scalar2=None, op0=ALU.add
+        )
+        std = keep.tile([P, 1], F32)
+        nc.scalar.activation(out=std[:], in_=var_eps[:], func=ACT.Sqrt)
+        rstd = keep.tile([P, 1], F32)
+        nc.vector.reciprocal(out=rstd[:], in_=std[:])
+        shift = keep.tile([P, 1], F32)
+        nc.vector.tensor_scalar(
+            out=shift[:],
+            in0=mean_var[:, 0:1],
+            scalar1=rstd[:, 0:1],
+            scalar2=-1.0,
+            op0=ALU.mult,
+            op1=ALU.mult,
+        )
+
+        def flip(sorted_rows):
+            flipped = flip_pool.tile([P, PACK, P], F32)
+            for t in range(PACK):
+                nc.tensor.transpose(
+                    out=flipped[:, t, :], in_=sorted_rows[:, t, :], identity=identity[:]
+                )
+            return flipped
+
+        gb_sorted = stage.tile([P, PACK, P], F32, tag="sorted")
+        nc.vector.tensor_copy(
+            out=gb_sorted[:], in_=gb_rows[:].rearrange("r (q t) -> r t q", t=PACK)
+        )
+        gb_flipped = flip(gb_sorted)
+        gain_bias = keep.tile([P, 2 * GROUPS, PACK], F32)
+        nc.vector.tensor_copy(
+            out=gain_bias[:], in_=gb_flipped[:, :, 0 : 2 * GROUPS].rearrange("p t r -> p r t")
+        )
+
+        pe_pairs = pe_sb[:].rearrange("p (j e) -> p j e", e=2)
+        own_factor = keep.tile([P, PAIRS, 2], F32)
+        nc.vector.tensor_copy(out=own_factor[:], in_=pe_pairs[:, :, 0:1].to_broadcast([P, PAIRS, 2]))
+        partner_factor = keep.tile([P, 2, PAIRS], F32)
+        nc.vector.tensor_scalar(
+            out=partner_factor[:, 0, :], in0=pe_pairs[:, :, 1], scalar1=-1.0, scalar2=None, op0=ALU.mult
+        )
+        nc.vector.tensor_copy(out=partner_factor[:, 1, :], in_=pe_pairs[:, :, 1])
+
+        h_codes = keep.tile([P, GROUPS, P], U32, align_bytes=64)
+        h_scales = keep.tile([P, GROUPS, P], U8, align_bytes=64)
+        acc = [acc_pool.tile([P, BANK], F32, name="acc%d" % c) for c in range(QK_BANKS + V_BANKS)]
+        sorted_x, flipped_x, grouped_h = {}, {}, {}
+
+        def normalise(g):
+            xn = stage.tile([P, PACK, P], F32, tag="sorted")
+            nc.scalar.activation(
+                out=xn[:],
+                in_=x_sb[:, g * K_PASS : (g + 1) * K_PASS].rearrange("r (q t) -> r t q", t=PACK),
+                func=ACT.Identity,
+                scale=rstd[:, 0:1],
+                bias=shift[:, 0:1],
+            )
+            sorted_x[g] = xn
+
+        def flip_group(g):
+            flipped_x[g] = flip(sorted_x[g])
+
+        def apply_gain_bias(g):
+            scaled = stage.tile([P, P, PACK], F32)
+            nc.vector.tensor_tensor(
+                out=scaled[:],
+                in0=flipped_x[g][:].rearrange("p t r -> p r t"),
+                in1=gain_bias[:, g, :].unsqueeze(1).to_broadcast([P, P, PACK]),
+                op=ALU.mult,
+            )
+            grouped = stage.tile([P, P, PACK], BF16, align_bytes=64)
+            nc.vector.tensor_tensor(
+                out=grouped[:],
+                in0=scaled[:],
+                in1=gain_bias[:, GROUPS + g, :].unsqueeze(1).to_broadcast([P, P, PACK]),
+                op=ALU.add,
+            )
+            grouped_h[g] = grouped
+
+        def project(g, words, first_bank, n_banks):
+            plane_rows = slice(SCALE_ROWS * (g % SHARE), P)
+            for c in range(n_banks):
+                bank = first_bank + c
+                nc.tensor.matmul_mx(
+                    out=acc[bank][:],
+                    lhsT=h_codes[:, g, :].bitcast(FP8X4),
+                    lhsT_scale=h_scales[:, g, :],
+                    rhs=words[:, c * BANK : (c + 1) * BANK].bitcast(FP8X4),
+                    rhs_scale=w_planes[plane_rows, g // SHARE, bank * BANK : (bank + 1) * BANK],
+                    start=(g == 0),
+                    stop=(g == GROUPS - 1),
+                )
+
+        def quantise_and_project(g):
+            nc.vector.quantize_mx(
+                out=h_codes[:, g, :].bitcast(FP8X4),
+                scales=h_scales[:, g, :],
+                in_=grouped_h[g][:].rearrange("p r t -> p (r t)"),
+            )
+            project(g, qk_words[g], 0, QK_BANKS)
+
+        stages = (normalise, flip_group, apply_gain_bias, quantise_and_project)
+        for step in range(GROUPS + len(stages) - 1):
+            for lag, run_stage in enumerate(stages):
+                g = step - lag
+                if 0 <= g < GROUPS:
+                    run_stage(g)
+
+        def store_bank(bank, values, queues):
+            which, half = divmod(bank, HEADS // BANK_HEADS)
+            heads = slice(half * BANK_HEADS, (half + 1) * BANK_HEADS)
+            for b in range(BATCH):
+                queues[b].dma_start(
+                    out=outs[which][b, heads].rearrange("h s d -> s h d"),
+                    in_=values[b * SEQ : (b + 1) * SEQ],
+                )
+
+        for bank in range(QK_BANKS):
+            pairs = acc[bank][:].rearrange("p (h j e) -> p h j e", j=PAIRS, e=2)
+            own = stage.tile([P, BANK_HEADS, PAIRS, 2], F32)
+            nc.vector.tensor_tensor(
+                out=own[:],
+                in0=pairs,
+                in1=own_factor[:].unsqueeze(1).to_broadcast([P, BANK_HEADS, PAIRS, 2]),
+                op=ALU.mult,
+            )
+            crossed = stage.tile([P, 2, BANK_HEADS, PAIRS], F32)
+            for e in range(2):
+                nc.vector.tensor_tensor(
+                    out=crossed[:, e],
+                    in0=pairs[:, :, :, 1 - e],
+                    in1=partner_factor[:, e, :].unsqueeze(1).to_broadcast([P, BANK_HEADS, PAIRS]),
+                    op=ALU.mult,
+                )
+            rotated = stage.tile([P, BANK_HEADS, PAIRS, 2], F32)
+            nc.vector.tensor_tensor(
+                out=rotated[:],
+                in0=own[:],
+                in1=crossed[:].rearrange("p e h j -> p h j e"),
+                op=ALU.add,
+            )
+            store_bank(bank, rotated[:].rearrange("p h j e -> p h (j e)"), (nc.scalar, nc.scalar))
+
+        for g in range(GROUPS):
+            project(g, v_words[g], QK_BANKS, V_BANKS)
+        for c, copy_out in enumerate((nc.scalar.copy, nc.vector.tensor_copy)):
+            values = stage.tile([P, BANK_HEADS, DH], F32, name="values%d" % c)
+            copy_out(out=values[:], in_=acc[QK_BANKS + c][:].rearrange("p (h d) -> p h d", d=DH))
+            store_bank(QK_BANKS + c, values[:], (nc.sync, nc.scalar))

@@ -74,17 +74,13 @@ def tile_minitransformerlayer_pa_k_kernel(
         for b in range(BATCH):
             nc.scalar.dma_start(out=pe_sb[b * SEQ : (b + 1) * SEQ, :], in_=pe)
 
-        scale_words = w_qkv_scales.bitcast(I32)
-        for a in range(GROUPS // SHARE):
-            for quadrant in range(QUADRANTS):
-                first = 32 * quadrant
-                nc.sync.dma_start(
-                    out=w_planes[first : first + SHARE * SCALE_ROWS, a, :].bitcast(I32),
-                    in_=scale_words[
-                        SHARE * a : SHARE * (a + 1),
-                        SCALE_ROWS * quadrant : SCALE_ROWS * (quadrant + 1),
-                        :,
-                    ],
+        scale_rows = w_qkv_scales.bitcast(F32).rearrange("(a i) q n -> q i a n", i=SHARE)
+        for quadrant in range(QUADRANTS):
+            for r in range(SCALE_ROWS):
+                first = 32 * quadrant + r
+                nc.gpsimd.dma_start(
+                    out=w_planes[first : first + SHARE * SCALE_ROWS : SCALE_ROWS].bitcast(F32),
+                    in_=scale_rows[SCALE_ROWS * quadrant + r],
                 )
 
         def load_words(pool, g, first_col, n_cols):

@@ -33,6 +33,8 @@ SHARE = 4
 X_PIECES = 4
 BN_STATS_DIM = 6
 QK_BUFS = 10
+SLACK = 2
+TAPER = 2
 
 FLOPS = 2 * P * D * N_COLS
 
@@ -47,7 +49,7 @@ def tile_minitransformerlayer_pa_k_kernel(
         keep = ctx.enter_context(tc.tile_pool(name="keep", bufs=1))
         stage = ctx.enter_context(tc.tile_pool(name="stage", bufs=2))
         qk_pool = ctx.enter_context(tc.tile_pool(name="qk_words", bufs=QK_BUFS))
-        v_pool = ctx.enter_context(tc.tile_pool(name="v_words", bufs=GROUPS))
+        v_pool = ctx.enter_context(tc.tile_pool(name="v_words", bufs=GROUPS + TAPER))
         acc_pool = ctx.enter_context(tc.psum_pool(name="acc", bufs=1))
         flip_pool = ctx.enter_context(tc.psum_pool(name="flip", bufs=2))
         ctx.enter_context(tc.manual_schedule())
@@ -74,13 +76,17 @@ def tile_minitransformerlayer_pa_k_kernel(
         for b in range(BATCH):
             nc.scalar.dma_start(out=pe_sb[b * SEQ : (b + 1) * SEQ, :], in_=pe)
 
-        scale_rows = w_qkv_scales.bitcast(F32).rearrange("(a i) q n -> q i a n", i=SHARE)
-        for quadrant in range(QUADRANTS):
-            for r in range(SCALE_ROWS):
-                first = 32 * quadrant + r
-                nc.gpsimd.dma_start(
-                    out=w_planes[first : first + SHARE * SCALE_ROWS : SCALE_ROWS].bitcast(F32),
-                    in_=scale_rows[SCALE_ROWS * quadrant + r],
+        scale_words = w_qkv_scales.bitcast(I32)
+        for a in range(GROUPS // SHARE):
+            for quadrant in range(QUADRANTS):
+                first = 32 * quadrant
+                nc.sync.dma_start(
+                    out=w_planes[first : first + SHARE * SCALE_ROWS, a, :].bitcast(I32),
+                    in_=scale_words[
+                        SHARE * a : SHARE * (a + 1),
+                        SCALE_ROWS * quadrant : SCALE_ROWS * (quadrant + 1),
+                        :,
+                    ],
                 )
 
         def load_words(pool, g, first_col, n_cols):
@@ -91,7 +97,11 @@ def tile_minitransformerlayer_pa_k_kernel(
             return words
 
         qk_words = [load_words(qk_pool, g, 0, QK_BANKS * BANK) for g in range(GROUPS)]
-        v_words = [load_words(v_pool, g, QK_BANKS * BANK, V_BANKS * BANK) for g in range(GROUPS)]
+        v_pieces = [(g, 0, V_BANKS) for g in range(GROUPS - TAPER)]
+        v_pieces += [(g, c, 1) for c in range(V_BANKS) for g in range(GROUPS - TAPER, GROUPS)]
+        v_words = [
+            load_words(v_pool, g, (QK_BANKS + c) * BANK, n_banks * BANK) for g, c, n_banks in v_pieces
+        ]
 
         stats = keep.tile([P, GROUPS, BN_STATS_DIM], F32)
         for g in range(GROUPS):
@@ -193,19 +203,21 @@ def tile_minitransformerlayer_pa_k_kernel(
                     stop=(g == GROUPS - 1),
                 )
 
-        def quantise_and_project(g):
+        def quantise(g):
             nc.vector.quantize_mx(
                 out=h_codes[:, g, :].bitcast(FP8X4),
                 scales=h_scales[:, g, :],
                 in_=grouped_h[g][:].rearrange("p r t -> p (r t)"),
             )
+
+        def project_qk(g):
             project(g, qk_words[g], 0, QK_BANKS)
 
-        stages = (normalise, flip_group, apply_gain_bias, quantise_and_project)
+        stages = (normalise, flip_group, apply_gain_bias, quantise) + SLACK * (None,) + (project_qk,)
         for step in range(GROUPS + len(stages) - 1):
             for lag, run_stage in enumerate(stages):
                 g = step - lag
-                if 0 <= g < GROUPS:
+                if run_stage is not None and 0 <= g < GROUPS:
                     run_stage(g)
 
         def store_bank(bank, values, queues):
@@ -243,8 +255,8 @@ def tile_minitransformerlayer_pa_k_kernel(
             )
             store_bank(bank, rotated[:].rearrange("p h j e -> p h (j e)"), (nc.scalar, nc.scalar))
 
-        for g in range(GROUPS):
-            project(g, v_words[g], QK_BANKS, V_BANKS)
+        for (g, c, n_banks), words in zip(v_pieces, v_words):
+            project(g, words, QK_BANKS + c, n_banks)
         for c, copy_out in enumerate((nc.scalar.copy, nc.vector.tensor_copy)):
             values = stage.tile([P, BANK_HEADS, DH], F32, name="values%d" % c)
             copy_out(out=values[:], in_=acc[QK_BANKS + c][:].rearrange("p (h d) -> p h d", d=DH))

@@ -32,7 +32,8 @@ QUADRANTS = 4
 SHARE = 4
 X_PIECES = 4
 BN_STATS_DIM = 6
-QK_BUFS = 10
+FULL_GROUPS = 8
+FULL_BUFS = 6
 SLACK = 2
 TAPER = 2
 
@@ -48,8 +49,11 @@ def tile_minitransformerlayer_pa_k_kernel(
     with ExitStack() as ctx:
         keep = ctx.enter_context(tc.tile_pool(name="keep", bufs=1))
         stage = ctx.enter_context(tc.tile_pool(name="stage", bufs=2))
-        qk_pool = ctx.enter_context(tc.tile_pool(name="qk_words", bufs=QK_BUFS))
-        v_pool = ctx.enter_context(tc.tile_pool(name="v_words", bufs=GROUPS + TAPER))
+        last = ctx.enter_context(tc.tile_pool(name="last", bufs=1))
+        full_pool = ctx.enter_context(tc.tile_pool(name="full_words", bufs=FULL_BUFS))
+        qk_pool = ctx.enter_context(tc.tile_pool(name="qk_words", bufs=GROUPS - FULL_GROUPS))
+        v_pool = ctx.enter_context(tc.tile_pool(name="v_words", bufs=GROUPS - FULL_GROUPS - TAPER))
+        taper_pool = ctx.enter_context(tc.tile_pool(name="taper_words", bufs=V_BANKS * TAPER))
         acc_pool = ctx.enter_context(tc.psum_pool(name="acc", bufs=1))
         flip_pool = ctx.enter_context(tc.psum_pool(name="flip", bufs=2))
         ctx.enter_context(tc.manual_schedule())
@@ -96,11 +100,15 @@ def tile_minitransformerlayer_pa_k_kernel(
             nc.sync.dma_start(out=words[:].bitcast(I32), in_=source.bitcast(I32))
             return words
 
-        qk_words = [load_words(qk_pool, g, 0, QK_BANKS * BANK) for g in range(GROUPS)]
-        v_pieces = [(g, 0, V_BANKS) for g in range(GROUPS - TAPER)]
+        main_words = [load_words(full_pool, g, 0, N_COLS) for g in range(FULL_GROUPS)]
+        main_words += [load_words(qk_pool, g, 0, QK_BANKS * BANK) for g in range(FULL_GROUPS, GROUPS)]
+        v_pieces = [(g, 0, V_BANKS) for g in range(FULL_GROUPS, GROUPS - TAPER)]
         v_pieces += [(g, c, 1) for c in range(V_BANKS) for g in range(GROUPS - TAPER, GROUPS)]
         v_words = [
-            load_words(v_pool, g, (QK_BANKS + c) * BANK, n_banks * BANK) for g, c, n_banks in v_pieces
+            load_words(
+                v_pool if n_banks == V_BANKS else taper_pool, g, (QK_BANKS + c) * BANK, n_banks * BANK
+            )
+            for g, c, n_banks in v_pieces
         ]
 
         stats = keep.tile([P, GROUPS, BN_STATS_DIM], F32)
@@ -210,10 +218,10 @@ def tile_minitransformerlayer_pa_k_kernel(
                 in_=grouped_h[g][:].rearrange("p r t -> p (r t)"),
             )
 
-        def project_qk(g):
-            project(g, qk_words[g], 0, QK_BANKS)
+        def project_main(g):
+            project(g, main_words[g], 0, QK_BANKS + V_BANKS if g < FULL_GROUPS else QK_BANKS)
 
-        stages = (normalise, flip_group, apply_gain_bias, quantise) + SLACK * (None,) + (project_qk,)
+        stages = (normalise, flip_group, apply_gain_bias, quantise) + SLACK * (None,) + (project_main,)
         for step in range(GROUPS + len(stages) - 1):
             for lag, run_stage in enumerate(stages):
                 g = step - lag
@@ -258,6 +266,6 @@ def tile_minitransformerlayer_pa_k_kernel(
         for (g, c, n_banks), words in zip(v_pieces, v_words):
             project(g, words, QK_BANKS + c, n_banks)
         for c, copy_out in enumerate((nc.scalar.copy, nc.vector.tensor_copy)):
-            values = stage.tile([P, BANK_HEADS, DH], F32, name="values%d" % c)
+            values = last.tile([P, BANK_HEADS, DH], F32, name="values%d" % c)
             copy_out(out=values[:], in_=acc[QK_BANKS + c][:].rearrange("p (h d) -> p h d", d=DH))
             store_bank(QK_BANKS + c, values[:], (nc.sync, nc.scalar))

@@ -59,9 +59,22 @@ def tile_minitransformerlayer_pa_k_kernel(
         ctx.enter_context(tc.manual_schedule())
 
         gb_rows = keep.tile([P, K_PASS], BF16)
-        nc.vector.memset(gb_rows[:], 0.0)
         w_planes = keep.tile([P, GROUPS // SHARE, N_COLS], U8, align_bytes=64)
         nc.vector.memset(w_planes[:].bitcast(I32), 0)
+        nc.vector.memset(gb_rows[:], 0.0)
+
+        scale_words = w_qkv_scales.bitcast(F32)
+        for a in range(GROUPS // SHARE):
+            for quadrant in range(QUADRANTS):
+                first = 32 * quadrant
+                nc.gpsimd.dma_start(
+                    out=w_planes[first : first + SHARE * SCALE_ROWS, a, :].bitcast(F32),
+                    in_=scale_words[
+                        SHARE * a : SHARE * (a + 1),
+                        SCALE_ROWS * quadrant : SCALE_ROWS * (quadrant + 1),
+                        :,
+                    ],
+                )
 
         identity = keep.tile([P, P], F32)
         make_identity(nc, identity[:])
@@ -79,19 +92,6 @@ def tile_minitransformerlayer_pa_k_kernel(
         pe_sb = keep.tile([P, DH], BF16)
         for b in range(BATCH):
             nc.scalar.dma_start(out=pe_sb[b * SEQ : (b + 1) * SEQ, :], in_=pe)
-
-        scale_words = w_qkv_scales.bitcast(I32)
-        for a in range(GROUPS // SHARE):
-            for quadrant in range(QUADRANTS):
-                first = 32 * quadrant
-                nc.sync.dma_start(
-                    out=w_planes[first : first + SHARE * SCALE_ROWS, a, :].bitcast(I32),
-                    in_=scale_words[
-                        SHARE * a : SHARE * (a + 1),
-                        SCALE_ROWS * quadrant : SCALE_ROWS * (quadrant + 1),
-                        :,
-                    ],
-                )
 
         def load_words(pool, g, first_col, n_cols):
             words = pool.tile([P, n_cols], U32, align_bytes=64)

@@ -63,6 +63,9 @@ def tile_minitransformerlayer_pa_k_kernel(
         nc.vector.memset(w_planes[:].bitcast(I32), 0)
         nc.vector.memset(gb_rows[:], 0.0)
 
+        identity = keep.tile([P, P], F32)
+        make_identity(nc, identity[:])
+
         scale_words = w_qkv_scales.bitcast(F32)
         for a in range(GROUPS // SHARE):
             for quadrant in range(QUADRANTS):
@@ -75,9 +78,6 @@ def tile_minitransformerlayer_pa_k_kernel(
                         :,
                     ],
                 )
-
-        identity = keep.tile([P, P], F32)
-        make_identity(nc, identity[:])
 
         x_rows = x.flatten_outer_dims()
         x_sb = keep.tile([P, D], BF16)

@@ -30,7 +30,7 @@ N_COLS = (QK_BANKS + V_BANKS) * BANK
 SCALE_ROWS = 4
 QUADRANTS = 4
 SHARE = 4
-X_PIECES = 4
+X_PIECES = 2
 BN_STATS_DIM = 6
 FULL_GROUPS = 8
 FULL_BUFS = 6
@@ -228,9 +228,8 @@ def tile_minitransformerlayer_pa_k_kernel(
                 if run_stage is not None and 0 <= g < GROUPS:
                     run_stage(g)
 
-        def store_bank(bank, values, queues):
-            which, half = divmod(bank, HEADS // BANK_HEADS)
-            heads = slice(half * BANK_HEADS, (half + 1) * BANK_HEADS)
+        def store_heads(which, first, n_heads, values, queues):
+            heads = slice(first, first + n_heads)
             for b in range(BATCH):
                 queues[b].dma_start(
                     out=outs[which][b, heads].rearrange("h s d -> s h d"),
@@ -261,11 +260,23 @@ def tile_minitransformerlayer_pa_k_kernel(
                 in1=crossed[:].rearrange("p e h j -> p h j e"),
                 op=ALU.add,
             )
-            store_bank(bank, rotated[:].rearrange("p h j e -> p h (j e)"), (nc.scalar, nc.scalar))
+            which, half = divmod(bank, HEADS // BANK_HEADS)
+            store_heads(
+                which,
+                half * BANK_HEADS,
+                BANK_HEADS,
+                rotated[:].rearrange("p h j e -> p h (j e)"),
+                (nc.scalar, nc.scalar),
+            )
 
         for (g, c, n_banks), words in zip(v_pieces, v_words):
             project(g, words, QK_BANKS + c, n_banks)
-        for c, copy_out in enumerate((nc.scalar.copy, nc.vector.tensor_copy)):
-            values = last.tile([P, BANK_HEADS, DH], F32, name="values%d" % c)
-            copy_out(out=values[:], in_=acc[QK_BANKS + c][:].rearrange("p (h d) -> p h d", d=DH))
-            store_bank(QK_BANKS + c, values[:], (nc.sync, nc.scalar))
+        for c, copy_out, n_heads in (
+            (0, nc.scalar.copy, BANK_HEADS),
+            (1, nc.vector.tensor_copy, BANK_HEADS // 2),
+        ):
+            bank = acc[QK_BANKS + c][:].rearrange("p (h d) -> p h d", d=DH)
+            for first in range(0, BANK_HEADS, n_heads):
+                values = last.tile([P, n_heads, DH], F32, name="values%d_%d" % (c, first))
+                copy_out(out=values[:], in_=bank[:, first : first + n_heads, :])
+                store_heads(2, c * BANK_HEADS + first, n_heads, values[:], (nc.sync, nc.scalar))

@@ -33,7 +33,6 @@ SHARE = 4
 X_PIECES = 2
 BN_STATS_DIM = 6
 FULL_GROUPS = 8
-FULL_BUFS = 6
 SLACK = 2
 TAPER = 2
 
@@ -50,9 +49,8 @@ def tile_minitransformerlayer_pa_k_kernel(
         keep = ctx.enter_context(tc.tile_pool(name="keep", bufs=1))
         stage = ctx.enter_context(tc.tile_pool(name="stage", bufs=2))
         last = ctx.enter_context(tc.tile_pool(name="last", bufs=1))
-        full_pool = ctx.enter_context(tc.tile_pool(name="full_words", bufs=FULL_BUFS))
+        full_pool = ctx.enter_context(tc.tile_pool(name="full_words", bufs=FULL_GROUPS))
         qk_pool = ctx.enter_context(tc.tile_pool(name="qk_words", bufs=GROUPS - FULL_GROUPS))
-        v_pool = ctx.enter_context(tc.tile_pool(name="v_words", bufs=GROUPS - FULL_GROUPS - TAPER))
         taper_pool = ctx.enter_context(tc.tile_pool(name="taper_words", bufs=V_BANKS * TAPER))
         acc_pool = ctx.enter_context(tc.psum_pool(name="acc", bufs=1))
         flip_pool = ctx.enter_context(tc.psum_pool(name="flip", bufs=2))
@@ -106,7 +104,7 @@ def tile_minitransformerlayer_pa_k_kernel(
         v_pieces += [(g, c, 1) for c in range(V_BANKS) for g in range(GROUPS - TAPER, GROUPS)]
         v_words = [
             load_words(
-                v_pool if n_banks == V_BANKS else taper_pool, g, (QK_BANKS + c) * BANK, n_banks * BANK
+                full_pool if n_banks == V_BANKS else taper_pool, g, (QK_BANKS + c) * BANK, n_banks * BANK
             )
             for g, c, n_banks in v_pieces
         ]

@@ -30,11 +30,13 @@ N_COLS = (QK_BANKS + V_BANKS) * BANK
 SCALE_ROWS = 4
 QUADRANTS = 4
 SHARE = 4
-X_PIECES = 2
+X_PIECES = 4
 BN_STATS_DIM = 6
 FULL_GROUPS = 8
 SLACK = 2
-TAPER = 2
+SINGLE_GROUPS = 4
+PAIR = 2
+TAPER = PAIR
 
 FLOPS = 2 * P * D * N_COLS
 
@@ -49,33 +51,39 @@ def tile_minitransformerlayer_pa_k_kernel(
         keep = ctx.enter_context(tc.tile_pool(name="keep", bufs=1))
         stage = ctx.enter_context(tc.tile_pool(name="stage", bufs=2))
         last = ctx.enter_context(tc.tile_pool(name="last", bufs=1))
-        full_pool = ctx.enter_context(tc.tile_pool(name="full_words", bufs=FULL_GROUPS))
-        qk_pool = ctx.enter_context(tc.tile_pool(name="qk_words", bufs=GROUPS - FULL_GROUPS))
-        taper_pool = ctx.enter_context(tc.tile_pool(name="taper_words", bufs=V_BANKS * TAPER))
+        full_pool = ctx.enter_context(tc.tile_pool(name="full_words", bufs=SINGLE_GROUPS))
+        full_pair_pool = ctx.enter_context(
+            tc.tile_pool(name="full_pair_words", bufs=(FULL_GROUPS - SINGLE_GROUPS) // PAIR)
+        )
+        qk_pool = ctx.enter_context(tc.tile_pool(name="qk_words", bufs=(GROUPS - FULL_GROUPS) // PAIR))
+        taper_pool = ctx.enter_context(tc.tile_pool(name="taper_words", bufs=V_BANKS))
         acc_pool = ctx.enter_context(tc.psum_pool(name="acc", bufs=1))
         flip_pool = ctx.enter_context(tc.psum_pool(name="flip", bufs=2))
         ctx.enter_context(tc.manual_schedule())
 
         gb_rows = keep.tile([P, K_PASS], BF16)
         w_planes = keep.tile([P, GROUPS // SHARE, N_COLS], U8, align_bytes=64)
-        nc.vector.memset(w_planes[:].bitcast(I32), 0)
+        for a in (2, 3, 0, 1):
+            nc.vector.memset(w_planes[:, a, :].bitcast(I32), 0)
         nc.vector.memset(gb_rows[:], 0.0)
 
         identity = keep.tile([P, P], F32)
         make_identity(nc, identity[:])
 
-        scale_words = w_qkv_scales.bitcast(F32)
-        for a in range(GROUPS // SHARE):
+        def load_scales(a, queue, word):
             for quadrant in range(QUADRANTS):
                 first = 32 * quadrant
-                nc.gpsimd.dma_start(
-                    out=w_planes[first : first + SHARE * SCALE_ROWS, a, :].bitcast(F32),
-                    in_=scale_words[
+                queue.dma_start(
+                    out=w_planes[first : first + SHARE * SCALE_ROWS, a, :].bitcast(word),
+                    in_=w_qkv_scales.bitcast(word)[
                         SHARE * a : SHARE * (a + 1),
                         SCALE_ROWS * quadrant : SCALE_ROWS * (quadrant + 1),
                         :,
                     ],
                 )
+
+        for a in (2, 3):
+            load_scales(a, nc.gpsimd, F32)
 
         x_rows = x.flatten_outer_dims()
         x_sb = keep.tile([P, D], BF16)
@@ -91,23 +99,31 @@ def tile_minitransformerlayer_pa_k_kernel(
         for b in range(BATCH):
             nc.scalar.dma_start(out=pe_sb[b * SEQ : (b + 1) * SEQ, :], in_=pe)
 
-        def load_words(pool, g, first_col, n_cols):
-            words = pool.tile([P, n_cols], U32, align_bytes=64)
-            source = w_qkv_words[g].rearrange("p n t -> p (n t)")
-            source = source[:, PACK * first_col : PACK * (first_col + n_cols)]
-            nc.sync.dma_start(out=words[:].bitcast(I32), in_=source.bitcast(I32))
-            return words
+        for a in (0, 1):
+            load_scales(a, nc.sync, I32)
 
-        main_words = [load_words(full_pool, g, 0, N_COLS) for g in range(FULL_GROUPS)]
-        main_words += [load_words(qk_pool, g, 0, QK_BANKS * BANK) for g in range(FULL_GROUPS, GROUPS)]
-        v_pieces = [(g, 0, V_BANKS) for g in range(FULL_GROUPS, GROUPS - TAPER)]
-        v_pieces += [(g, c, 1) for c in range(V_BANKS) for g in range(GROUPS - TAPER, GROUPS)]
-        v_words = [
-            load_words(
-                full_pool if n_banks == V_BANKS else taper_pool, g, (QK_BANKS + c) * BANK, n_banks * BANK
-            )
-            for g, c, n_banks in v_pieces
-        ]
+        words_of = {}
+
+        def load_words(pool, first_group, n_groups, first_bank, n_banks):
+            words = pool.tile([P, n_groups, n_banks * BANK], U32, align_bytes=64)
+            first = PACK * BANK * first_bank
+            source = w_qkv_words[first_group : first_group + n_groups].rearrange("g p n t -> p g (n t)")
+            source = source[:, :, first : first + PACK * BANK * n_banks]
+            nc.sync.dma_start(out=words[:].bitcast(I32), in_=source.bitcast(I32))
+            for i in range(n_groups):
+                for c in range(n_banks):
+                    words_of[first_group + i, first_bank + c] = words[:, i, c * BANK : (c + 1) * BANK]
+
+        for g in range(SINGLE_GROUPS):
+            load_words(full_pool, g, 1, 0, QK_BANKS + V_BANKS)
+        for g in range(SINGLE_GROUPS, FULL_GROUPS, PAIR):
+            load_words(full_pair_pool, g, PAIR, 0, QK_BANKS + V_BANKS)
+        for g in range(FULL_GROUPS, GROUPS, PAIR):
+            load_words(qk_pool, g, PAIR, 0, QK_BANKS)
+        for g in range(FULL_GROUPS, GROUPS - TAPER, PAIR):
+            load_words(full_pool, g, PAIR, QK_BANKS, V_BANKS)
+        for c in range(V_BANKS):
+            load_words(taper_pool, GROUPS - TAPER, TAPER, QK_BANKS + c, 1)
 
         stats = keep.tile([P, GROUPS, BN_STATS_DIM], F32)
         for g in range(GROUPS):
@@ -179,7 +195,7 @@ def tile_minitransformerlayer_pa_k_kernel(
             flipped_x[g] = flip(sorted_x[g])
 
         def apply_gain_bias(g):
-            scaled = stage.tile([P, P, PACK], F32)
+            scaled = stage.tile([P, P, PACK], F32, tag="scaled")
             nc.vector.tensor_tensor(
                 out=scaled[:],
                 in0=flipped_x[g][:].rearrange("p t r -> p r t"),
@@ -195,15 +211,14 @@ def tile_minitransformerlayer_pa_k_kernel(
             )
             grouped_h[g] = grouped
 
-        def project(g, words, first_bank, n_banks):
+        def project(g, banks):
             plane_rows = slice(SCALE_ROWS * (g % SHARE), P)
-            for c in range(n_banks):
-                bank = first_bank + c
+            for bank in banks:
                 nc.tensor.matmul_mx(
                     out=acc[bank][:],
                     lhsT=h_codes[:, g, :].bitcast(FP8X4),
                     lhsT_scale=h_scales[:, g, :],
-                    rhs=words[:, c * BANK : (c + 1) * BANK].bitcast(FP8X4),
+                    rhs=words_of[g, bank].bitcast(FP8X4),
                     rhs_scale=w_planes[plane_rows, g // SHARE, bank * BANK : (bank + 1) * BANK],
                     start=(g == 0),
                     stop=(g == GROUPS - 1),
@@ -217,7 +232,7 @@ def tile_minitransformerlayer_pa_k_kernel(
             )
 
         def project_main(g):
-            project(g, main_words[g], 0, QK_BANKS + V_BANKS if g < FULL_GROUPS else QK_BANKS)
+            project(g, range(QK_BANKS + V_BANKS if g < FULL_GROUPS else QK_BANKS))
 
         stages = (normalise, flip_group, apply_gain_bias, quantise) + SLACK * (None,) + (project_main,)
         for step in range(GROUPS + len(stages) - 1):
@@ -235,8 +250,11 @@ def tile_minitransformerlayer_pa_k_kernel(
                 )
 
         for bank in range(QK_BANKS):
+            which, half = divmod(bank, HEADS // BANK_HEADS)
+            if half == 0:
+                rotated = stage.tile([P, HEADS, PAIRS, 2], F32)
             pairs = acc[bank][:].rearrange("p (h j e) -> p h j e", j=PAIRS, e=2)
-            own = stage.tile([P, BANK_HEADS, PAIRS, 2], F32)
+            own = stage.tile([P, BANK_HEADS, PAIRS, 2], F32, tag="scaled")
             nc.vector.tensor_tensor(
                 out=own[:],
                 in0=pairs,
@@ -251,24 +269,23 @@ def tile_minitransformerlayer_pa_k_kernel(
                     in1=partner_factor[:, e, :].unsqueeze(1).to_broadcast([P, BANK_HEADS, PAIRS]),
                     op=ALU.mult,
                 )
-            rotated = stage.tile([P, BANK_HEADS, PAIRS, 2], F32)
             nc.vector.tensor_tensor(
-                out=rotated[:],
+                out=rotated[:, half * BANK_HEADS : (half + 1) * BANK_HEADS],
                 in0=own[:],
                 in1=crossed[:].rearrange("p e h j -> p h j e"),
                 op=ALU.add,
             )
-            which, half = divmod(bank, HEADS // BANK_HEADS)
-            store_heads(
-                which,
-                half * BANK_HEADS,
-                BANK_HEADS,
-                rotated[:].rearrange("p h j e -> p h (j e)"),
-                (nc.scalar, nc.scalar),
-            )
+            if which == 1 or half == 1:
+                first = half * BANK_HEADS if which == 1 else 0
+                end = (half + 1) * BANK_HEADS
+                values = rotated[:, first:end].rearrange("p h j e -> p h (j e)")
+                store_heads(which, first, end - first, values, (nc.scalar, nc.scalar))
 
-        for (g, c, n_banks), words in zip(v_pieces, v_words):
-            project(g, words, QK_BANKS + c, n_banks)
+        for g in range(FULL_GROUPS, GROUPS - TAPER):
+            project(g, range(QK_BANKS, QK_BANKS + V_BANKS))
+        for bank in range(QK_BANKS, QK_BANKS + V_BANKS):
+            for g in range(GROUPS - TAPER, GROUPS):
+                project(g, (bank,))
         for c, copy_out, n_heads in (
             (0, nc.scalar.copy, BANK_HEADS),
             (1, nc.vector.tensor_copy, BANK_HEADS // 2),

from contextlib import ExitStack

import concourse.mybir as mybir
from concourse.masks import make_identity

F32 = mybir.dt.float32
BF16 = mybir.dt.bfloat16
I32 = mybir.dt.int32
U32 = mybir.dt.uint32
U8 = mybir.dt.uint8
FP8X4 = mybir.dt.float8_e4m3fn_x4
ALU = mybir.AluOpType
ACT = mybir.ActivationFunctionType

P = 128
PACK = 4
K_PASS = P * PACK
BATCH, SEQ, D = 2, 64, 8192
HEADS, DH = 16, 64
PAIRS = DH // 2
GROUPS = D // K_PASS
EPS = 1e-5

BANK = 512
BANK_HEADS = BANK // DH
QK_BANKS = 2 * HEADS * DH // BANK
V_BANKS = HEADS * DH // BANK
N_COLS = (QK_BANKS + V_BANKS) * BANK

SCALE_ROWS = 4
QUADRANTS = 4
SHARE = 4
X_PIECES = 4
BN_STATS_DIM = 6
FULL_GROUPS = 8
SLACK = 2
SINGLE_GROUPS = 4
PAIR = 2
TAPER = PAIR

FLOPS = 2 * P * D * N_COLS


def tile_minitransformerlayer_pa_k_kernel(
    tc, x, pe, w_qkv_words, w_qkv_scales, g1, b1, out_0, out_1, out_2
):
    nc = tc.nc
    outs = (out_0, out_1, out_2)

    with ExitStack() as ctx:
        keep = ctx.enter_context(tc.tile_pool(name="keep", bufs=1))
        stage = ctx.enter_context(tc.tile_pool(name="stage", bufs=2))
        last = ctx.enter_context(tc.tile_pool(name="last", bufs=1))
        full_pool = ctx.enter_context(tc.tile_pool(name="full_words", bufs=SINGLE_GROUPS))
        full_pair_pool = ctx.enter_context(
            tc.tile_pool(name="full_pair_words", bufs=(FULL_GROUPS - SINGLE_GROUPS) // PAIR)
        )
        qk_pool = ctx.enter_context(tc.tile_pool(name="qk_words", bufs=(GROUPS - FULL_GROUPS) // PAIR))
        taper_pool = ctx.enter_context(tc.tile_pool(name="taper_words", bufs=V_BANKS))
        acc_pool = ctx.enter_context(tc.psum_pool(name="acc", bufs=1))
        flip_pool = ctx.enter_context(tc.psum_pool(name="flip", bufs=2))
        ctx.enter_context(tc.manual_schedule())

        gb_rows = keep.tile([P, K_PASS], BF16)
        w_planes = keep.tile([P, GROUPS // SHARE, N_COLS], U8, align_bytes=64)
        for a in (2, 3, 0, 1):
            nc.vector.memset(w_planes[:, a, :].bitcast(I32), 0)
        nc.vector.memset(gb_rows[:], 0.0)

        identity = keep.tile([P, P], F32)
        make_identity(nc, identity[:])

        def load_scales(a, queue, word):
            for quadrant in range(QUADRANTS):
                first = 32 * quadrant
                queue.dma_start(
                    out=w_planes[first : first + SHARE * SCALE_ROWS, a, :].bitcast(word),
                    in_=w_qkv_scales.bitcast(word)[
                        SHARE * a : SHARE * (a + 1),
                        SCALE_ROWS * quadrant : SCALE_ROWS * (quadrant + 1),
                        :,
                    ],
                )

        for a in (2, 3):
            load_scales(a, nc.gpsimd, F32)

        x_rows = x.flatten_outer_dims()
        x_sb = keep.tile([P, D], BF16)
        for piece in range(X_PIECES):
            cols = slice(piece * D // X_PIECES, (piece + 1) * D // X_PIECES)
            nc.sync.dma_start(out=x_sb[:, cols], in_=x_rows[:, cols])

        nc.scalar.dma_start(out=gb_rows[0:GROUPS, :], in_=g1.rearrange("(g k) -> g k", k=K_PASS))
        nc.scalar.dma_start(
            out=gb_rows[GROUPS : 2 * GROUPS, :], in_=b1.rearrange("(g k) -> g k", k=K_PASS)
        )
        pe_sb = keep.tile([P, DH], BF16)
        for b in range(BATCH):
            nc.scalar.dma_start(out=pe_sb[b * SEQ : (b + 1) * SEQ, :], in_=pe)

        for a in (0, 1):
            load_scales(a, nc.sync, I32)

        words_of = {}

        def load_words(pool, first_group, n_groups, first_bank, n_banks):
            words = pool.tile([P, n_groups, n_banks * BANK], U32, align_bytes=64)
            first = PACK * BANK * first_bank
            source = w_qkv_words[first_group : first_group + n_groups].rearrange("g p n t -> p g (n t)")
            source = source[:, :, first : first + PACK * BANK * n_banks]
            nc.sync.dma_start(out=words[:].bitcast(I32), in_=source.bitcast(I32))
            for i in range(n_groups):
                for c in range(n_banks):
                    words_of[first_group + i, first_bank + c] = words[:, i, c * BANK : (c + 1) * BANK]

        for g in range(SINGLE_GROUPS):
            load_words(full_pool, g, 1, 0, QK_BANKS + V_BANKS)
        for g in range(SINGLE_GROUPS, FULL_GROUPS, PAIR):
            load_words(full_pair_pool, g, PAIR, 0, QK_BANKS + V_BANKS)
        for g in range(FULL_GROUPS, GROUPS, PAIR):
            load_words(qk_pool, g, PAIR, 0, QK_BANKS)
        for g in range(FULL_GROUPS, GROUPS - TAPER, PAIR):
            load_words(full_pool, g, PAIR, QK_BANKS, V_BANKS)
        for c in range(V_BANKS):
            load_words(taper_pool, GROUPS - TAPER, TAPER, QK_BANKS + c, 1)

        stats = keep.tile([P, GROUPS, BN_STATS_DIM], F32)
        for g in range(GROUPS):
            nc.vector.bn_stats(out=stats[:, g, :], in_=x_sb[:, g * K_PASS : (g + 1) * K_PASS])
        mean_var = keep.tile([P, 2], F32)
        nc.vector.bn_aggr(out=mean_var[:], in_=stats[:].rearrange("p g s -> p (g s)"))
        var_eps = keep.tile([P, 1], F32)
        nc.vector.tensor_scalar(
            out=var_eps[:], in0=mean_var[:, 1:2], scalar1=EPS, scalar2=None, op0=ALU.add
        )
        std = keep.tile([P, 1], F32)
        nc.scalar.activation(out=std[:], in_=var_eps[:], func=ACT.Sqrt)
        rstd = keep.tile([P, 1], F32)
        nc.vector.reciprocal(out=rstd[:], in_=std[:])
        shift = keep.tile([P, 1], F32)
        nc.vector.tensor_scalar(
            out=shift[:],
            in0=mean_var[:, 0:1],
            scalar1=rstd[:, 0:1],
            scalar2=-1.0,
            op0=ALU.mult,
            op1=ALU.mult,
        )

        def flip(sorted_rows):
            flipped = flip_pool.tile([P, PACK, P], F32)
            for t in range(PACK):
                nc.tensor.transpose(
                    out=flipped[:, t, :], in_=sorted_rows[:, t, :], identity=identity[:]
                )
            return flipped

        gb_sorted = stage.tile([P, PACK, P], F32, tag="sorted")
        nc.vector.tensor_copy(
            out=gb_sorted[:], in_=gb_rows[:].rearrange("r (q t) -> r t q", t=PACK)
        )
        gb_flipped = flip(gb_sorted)
        gain_bias = keep.tile([P, 2 * GROUPS, PACK], F32)
        nc.vector.tensor_copy(
            out=gain_bias[:], in_=gb_flipped[:, :, 0 : 2 * GROUPS].rearrange("p t r -> p r t")
        )

        pe_pairs = pe_sb[:].rearrange("p (j e) -> p j e", e=2)
        own_factor = keep.tile([P, PAIRS, 2], F32)
        nc.vector.tensor_copy(out=own_factor[:], in_=pe_pairs[:, :, 0:1].to_broadcast([P, PAIRS, 2]))
        partner_factor = keep.tile([P, 2, PAIRS], F32)
        nc.vector.tensor_scalar(
            out=partner_factor[:, 0, :], in0=pe_pairs[:, :, 1], scalar1=-1.0, scalar2=None, op0=ALU.mult
        )
        nc.vector.tensor_copy(out=partner_factor[:, 1, :], in_=pe_pairs[:, :, 1])

        h_codes = keep.tile([P, GROUPS, P], U32, align_bytes=64)
        h_scales = keep.tile([P, GROUPS, P], U8, align_bytes=64)
        acc = [acc_pool.tile([P, BANK], F32, name="acc%d" % c) for c in range(QK_BANKS + V_BANKS)]
        sorted_x, flipped_x, grouped_h = {}, {}, {}

        def normalise(g):
            xn = stage.tile([P, PACK, P], F32, tag="sorted")
            nc.scalar.activation(
                out=xn[:],
                in_=x_sb[:, g * K_PASS : (g + 1) * K_PASS].rearrange("r (q t) -> r t q", t=PACK),
                func=ACT.Identity,
                scale=rstd[:, 0:1],
                bias=shift[:, 0:1],
            )
            sorted_x[g] = xn

        def flip_group(g):
            flipped_x[g] = flip(sorted_x[g])

        def apply_gain_bias(g):
            scaled = stage.tile([P, P, PACK], F32, tag="scaled")
            nc.vector.tensor_tensor(
                out=scaled[:],
                in0=flipped_x[g][:].rearrange("p t r -> p r t"),
                in1=gain_bias[:, g, :].unsqueeze(1).to_broadcast([P, P, PACK]),
                op=ALU.mult,
            )
            grouped = stage.tile([P, P, PACK], BF16, align_bytes=64)
            nc.vector.tensor_tensor(
                out=grouped[:],
                in0=scaled[:],
                in1=gain_bias[:, GROUPS + g, :].unsqueeze(1).to_broadcast([P, P, PACK]),
                op=ALU.add,
            )
            grouped_h[g] = grouped

        def project(g, banks):
            plane_rows = slice(SCALE_ROWS * (g % SHARE), P)
            for bank in banks:
                nc.tensor.matmul_mx(
                    out=acc[bank][:],
                    lhsT=h_codes[:, g, :].bitcast(FP8X4),
                    lhsT_scale=h_scales[:, g, :],
                    rhs=words_of[g, bank].bitcast(FP8X4),
                    rhs_scale=w_planes[plane_rows, g // SHARE, bank * BANK : (bank + 1) * BANK],
                    start=(g == 0),
                    stop=(g == GROUPS - 1),
                )

        def quantise(g):
            nc.vector.quantize_mx(
                out=h_codes[:, g, :].bitcast(FP8X4),
                scales=h_scales[:, g, :],
                in_=grouped_h[g][:].rearrange("p r t -> p (r t)"),
            )

        def project_main(g):
            project(g, range(QK_BANKS + V_BANKS if g < FULL_GROUPS else QK_BANKS))

        stages = (normalise, flip_group, apply_gain_bias, quantise) + SLACK * (None,) + (project_main,)
        for step in range(GROUPS + len(stages) - 1):
            for lag, run_stage in enumerate(stages):
                g = step - lag
                if run_stage is not None and 0 <= g < GROUPS:
                    run_stage(g)

        def store_heads(which, first, n_heads, values, queues):
            heads = slice(first, first + n_heads)
            for b in range(BATCH):
                queues[b].dma_start(
                    out=outs[which][b, heads].rearrange("h s d -> s h d"),
                    in_=values[b * SEQ : (b + 1) * SEQ],
                )

        for bank in range(QK_BANKS):
            which, half = divmod(bank, HEADS // BANK_HEADS)
            if half == 0:
                rotated = stage.tile([P, HEADS, PAIRS, 2], F32)
            pairs = acc[bank][:].rearrange("p (h j e) -> p h j e", j=PAIRS, e=2)
            own = stage.tile([P, BANK_HEADS, PAIRS, 2], F32, tag="scaled")
            nc.vector.tensor_tensor(
                out=own[:],
                in0=pairs,
                in1=own_factor[:].unsqueeze(1).to_broadcast([P, BANK_HEADS, PAIRS, 2]),
                op=ALU.mult,
            )
            crossed = stage.tile([P, 2, BANK_HEADS, PAIRS], F32)
            for e in range(2):
                nc.vector.tensor_tensor(
                    out=crossed[:, e],
                    in0=pairs[:, :, :, 1 - e],
                    in1=partner_factor[:, e, :].unsqueeze(1).to_broadcast([P, BANK_HEADS, PAIRS]),
                    op=ALU.mult,
                )
            nc.vector.tensor_tensor(
                out=rotated[:, half * BANK_HEADS : (half + 1) * BANK_HEADS],
                in0=own[:],
                in1=crossed[:].rearrange("p e h j -> p h j e"),
                op=ALU.add,
            )
            if which == 1 or half == 1:
                first = half * BANK_HEADS if which == 1 else 0
                end = (half + 1) * BANK_HEADS
                values = rotated[:, first:end].rearrange("p h j e -> p h (j e)")
                store_heads(which, first, end - first, values, (nc.scalar, nc.scalar))

        for g in range(FULL_GROUPS, GROUPS - TAPER):
            project(g, range(QK_BANKS, QK_BANKS + V_BANKS))
        for bank in range(QK_BANKS, QK_BANKS + V_BANKS):
            for g in range(GROUPS - TAPER, GROUPS):
                project(g, (bank,))
        for c, copy_out, n_heads in (
            (0, nc.scalar.copy, BANK_HEADS),
            (1, nc.vector.tensor_copy, BANK_HEADS // 2),
        ):
            bank = acc[QK_BANKS + c][:].rearrange("p (h d) -> p h d", d=DH)
            for first in range(0, BANK_HEADS, n_heads):
                values = last.tile([P, n_heads, DH], F32, name="values%d_%d" % (c, first))
                copy_out(out=values[:], in_=bank[:, first : first + n_heads, :])
                store_heads(2, c * BANK_HEADS + first, n_heads, values[:], (nc.sync, nc.scalar))
